import numpy as np
import ml_dtypes

BF16 = ml_dtypes.bfloat16


def bf(x):
    return np.asarray(x, np.float32).astype(BF16)


def f32(x):
    return np.asarray(x, np.float32)


def f64(x):
    return np.asarray(x).astype(np.float64)


def striped(idx):
    return np.tile(idx.reshape(-1, 16).T, (8, 1))


C, S, KV, N = 128, 4096, 128, 2048
EPS = 1e-5


def setup_inputs():
    return {
        "img": bf(np.random.standard_normal((C, S))),
        "gamma": f32(1.0 + 0.1 * np.random.standard_normal((C, 1))),
        "beta": f32(0.1 * np.random.standard_normal((C, 1))),
        "w_kv": bf(np.random.standard_normal((C, KV)) / np.sqrt(C)),
        "b_kv": f32(0.1 * np.random.standard_normal((KV, 1))),
        "offs": striped(np.random.permutation(np.tile(np.arange(S), 2))[:N]),
    }


def reference(img, gamma, beta, w_kv, b_kv, offs):
    idx = offs[:16].T.reshape(-1)
    xn = f64(gamma) * f64(img) * (1.0 / np.sqrt(1.0 + EPS)) + f64(beta)
    picked = xn[:, idx]
    kv = f64(w_kv).T @ picked + f64(b_kv)
    return np.concatenate([kv, picked], axis=0)

@@ -1,0 +1,75 @@
+import math
+
+import concourse.mybir as mybir
+from concourse.masks import make_identity
+
+C, S, KV, N = 128, 4096, 128, 2048
+EPS = 1e-5
+INV_STD = 1.0 / math.sqrt(1.0 + EPS)
+
+PIECE = 512
+N_PIECES = N // PIECE
+PIECE_COLS = PIECE // 16
+CHUNK = 1024
+N_CHUNKS = S // CHUNK
+
+FLOPS = 2 * C * KV * N
+
+BF16, F32, U16 = mybir.dt.bfloat16, mybir.dt.float32, mybir.dt.uint16
+MULT, ADD = mybir.AluOpType.mult, mybir.AluOpType.add
+IDENTITY = mybir.ActivationFunctionType.Identity
+
+
+def tile_pointnet2msg_kernel(tc, img, gamma, beta, w_kv, b_kv, offs, out):
+    nc = tc.nc
+    with (
+        tc.tile_pool(name="held", bufs=1) as held,
+        tc.tile_pool(name="staged", bufs=N_PIECES) as staged,
+        tc.psum_pool(name="banks", bufs=N_PIECES) as banks,
+    ):
+        gamma_t = held.tile([C, 1], F32, name="gamma_t")
+        beta_t = held.tile([C, 1], F32, name="beta_t")
+        nc.scalar.dma_start(gamma_t[:], gamma)
+        nc.scalar.dma_start(beta_t[:], beta)
+
+        raw = []
+        for k in range(N_CHUNKS):
+            chunk = held.tile([C, CHUNK], BF16, name=f"raw{k}")
+            queue = nc.sync if k % 2 == 0 else nc.scalar
+            queue.dma_start(chunk[:], img[:, k * CHUNK : (k + 1) * CHUNK])
+            raw.append(chunk)
+
+        offsets = held.tile([128, N // 16], U16, name="offsets")
+        nc.sync.dma_start(offsets[:], offs)
+
+        weights = held.tile([C, KV], BF16, name="weights")
+        bias_t = held.tile([KV, 1], F32, name="bias_t")
+        nc.gpsimd.dma_start(weights[:], w_kv)
+        nc.gpsimd.dma_start(bias_t[:], b_kv)
+
+        identity = held.tile([C, C], BF16, name="identity")
+        make_identity(nc, identity[:])
+
+        scale_t = held.tile([C, 1], F32, name="scale_t")
+        nc.vector.tensor_scalar_mul(scale_t[:], gamma_t[:], INV_STD)
+        xn = held.tile([C, S], BF16, name="xn")
+        for k in range(N_CHUNKS):
+            nc.vector.tensor_scalar(
+                xn[:, k * CHUNK : (k + 1) * CHUNK], raw[k][:], scale_t[:], beta_t[:], MULT, ADD
+            )
+
+        for j in range(N_PIECES):
+            picked_cols = xn[:].indirect(offsets[:, j * PIECE_COLS : (j + 1) * PIECE_COLS])
+            cols = slice(j * PIECE, (j + 1) * PIECE)
+
+            kv_bank = banks.tile([KV, PIECE], F32, name="kv_bank")
+            nc.tensor.matmul(kv_bank[:], weights[:], picked_cols, start=True, stop=True)
+            kv_out = staged.tile([KV, PIECE], F32, name="kv_out")
+            nc.scalar.activation(kv_out[:], kv_bank[:], IDENTITY, bias=bias_t[:])
+            nc.sync.dma_start(out[0:KV, cols], kv_out[:])
+
+            xn_bank = banks.tile([C, PIECE], F32, name="xn_bank")
+            nc.tensor.matmul(xn_bank[:], identity[:], picked_cols, start=True, stop=True)
+            xn_out = staged.tile([C, PIECE], F32, name="xn_out")
+            nc.vector.tensor_copy(xn_out[:], xn_bank[:])
+            nc.sync.dma_start(out[KV : KV + C, cols], xn_out[:])

@@ -44,8 +44,8 @@ def tile_pointnet2msg_kernel(tc, img, gamma, beta, w_kv, b_kv, offs, out):
 
         weights = held.tile([C, KV], BF16, name="weights")
         bias_t = held.tile([KV, 1], F32, name="bias_t")
-        nc.gpsimd.dma_start(weights[:], w_kv)
-        nc.gpsimd.dma_start(bias_t[:], b_kv)
+        nc.scalar.dma_start(weights[:], w_kv)
+        nc.sync.dma_start(bias_t[:], b_kv)
 
         identity = held.tile([C, C], BF16, name="identity")
         make_identity(nc, identity[:])

@@ -12,6 +12,7 @@ N_PIECES = N // PIECE
 PIECE_COLS = PIECE // 16
 CHUNK = 1024
 N_CHUNKS = S // CHUNK
+IDLE_WARMUPS = 6
 
 FLOPS = 2 * C * KV * N
 
@@ -25,8 +26,15 @@ def tile_pointnet2msg_kernel(tc, img, gamma, beta, w_kv, b_kv, offs, out):
     with (
         tc.tile_pool(name="held", bufs=1) as held,
         tc.tile_pool(name="staged", bufs=N_PIECES) as staged,
-        tc.psum_pool(name="banks", bufs=N_PIECES) as banks,
+        tc.psum_pool(name="banks", bufs=3) as banks,
+        tc.psum_pool(name="warm", bufs=1) as warm,
     ):
+        zeros = held.tile([C, PIECE], BF16, name="zeros")
+        nc.vector.memset(zeros[:], 0.0)
+        warm_bank = warm.tile([C, PIECE], F32, name="warm_bank")
+        for i in range(IDLE_WARMUPS):
+            nc.tensor.matmul(warm_bank[:], zeros[:, 0:C], zeros[:], start=True, stop=True)
+
         gamma_t = held.tile([C, 1], F32, name="gamma_t")
         beta_t = held.tile([C, 1], F32, name="beta_t")
         nc.scalar.dma_start(gamma_t[:], gamma)
@@ -44,8 +52,8 @@ def tile_pointnet2msg_kernel(tc, img, gamma, beta, w_kv, b_kv, offs, out):
 
         weights = held.tile([C, KV], BF16, name="weights")
         bias_t = held.tile([KV, 1], F32, name="bias_t")
-        nc.scalar.dma_start(weights[:], w_kv)
-        nc.sync.dma_start(bias_t[:], b_kv)
+        nc.gpsimd.dma_start(weights[:], w_kv)
+        nc.gpsimd.dma_start(bias_t[:], b_kv)
 
         identity = held.tile([C, C], BF16, name="identity")
         make_identity(nc, identity[:])
@@ -57,6 +65,8 @@ def tile_pointnet2msg_kernel(tc, img, gamma, beta, w_kv, b_kv, offs, out):
             nc.vector.tensor_scalar(
                 xn[:, k * CHUNK : (k + 1) * CHUNK], raw[k][:], scale_t[:], beta_t[:], MULT, ADD
             )
+            if k < N_CHUNKS - 1:
+                nc.tensor.matmul(warm_bank[:], zeros[:, 0:C], raw[k][:, 0:PIECE], start=True, stop=True)
 
         for j in range(N_PIECES):
             picked_cols = xn[:].indirect(offsets[:, j * PIECE_COLS : (j + 1) * PIECE_COLS])

@@ -12,7 +12,6 @@ N_PIECES = N // PIECE
 PIECE_COLS = PIECE // 16
 CHUNK = 1024
 N_CHUNKS = S // CHUNK
-IDLE_WARMUPS = 6
 
 FLOPS = 2 * C * KV * N
 
@@ -26,15 +25,8 @@ def tile_pointnet2msg_kernel(tc, img, gamma, beta, w_kv, b_kv, offs, out):
     with (
         tc.tile_pool(name="held", bufs=1) as held,
         tc.tile_pool(name="staged", bufs=N_PIECES) as staged,
-        tc.psum_pool(name="banks", bufs=3) as banks,
-        tc.psum_pool(name="warm", bufs=1) as warm,
+        tc.psum_pool(name="banks", bufs=N_PIECES) as banks,
     ):
-        zeros = held.tile([C, PIECE], BF16, name="zeros")
-        nc.vector.memset(zeros[:], 0.0)
-        warm_bank = warm.tile([C, PIECE], F32, name="warm_bank")
-        for i in range(IDLE_WARMUPS):
-            nc.tensor.matmul(warm_bank[:], zeros[:, 0:C], zeros[:], start=True, stop=True)
-
         gamma_t = held.tile([C, 1], F32, name="gamma_t")
         beta_t = held.tile([C, 1], F32, name="beta_t")
         nc.scalar.dma_start(gamma_t[:], gamma)
@@ -65,21 +57,23 @@ def tile_pointnet2msg_kernel(tc, img, gamma, beta, w_kv, b_kv, offs, out):
             nc.vector.tensor_scalar(
                 xn[:, k * CHUNK : (k + 1) * CHUNK], raw[k][:], scale_t[:], beta_t[:], MULT, ADD
             )
-            if k < N_CHUNKS - 1:
-                nc.tensor.matmul(warm_bank[:], zeros[:, 0:C], raw[k][:, 0:PIECE], start=True, stop=True)
 
         for j in range(N_PIECES):
             picked_cols = xn[:].indirect(offsets[:, j * PIECE_COLS : (j + 1) * PIECE_COLS])
             cols = slice(j * PIECE, (j + 1) * PIECE)
 
             kv_bank = banks.tile([KV, PIECE], F32, name="kv_bank")
-            nc.tensor.matmul(kv_bank[:], weights[:], picked_cols, start=True, stop=True)
-            kv_out = staged.tile([KV, PIECE], F32, name="kv_out")
-            nc.scalar.activation(kv_out[:], kv_bank[:], IDENTITY, bias=bias_t[:])
-            nc.sync.dma_start(out[0:KV, cols], kv_out[:])
-
             xn_bank = banks.tile([C, PIECE], F32, name="xn_bank")
+            nc.tensor.matmul(kv_bank[:], weights[:], picked_cols, start=True, stop=True)
             nc.tensor.matmul(xn_bank[:], identity[:], picked_cols, start=True, stop=True)
+
+            kv_out = staged.tile([KV, PIECE], F32, name="kv_out")
             xn_out = staged.tile([C, PIECE], F32, name="xn_out")
-            nc.vector.tensor_copy(xn_out[:], xn_bank[:])
+            if j % 2 == 0:
+                nc.scalar.activation(kv_out[:], kv_bank[:], IDENTITY, bias=bias_t[:])
+                nc.vector.tensor_copy(xn_out[:], xn_bank[:])
+            else:
+                nc.vector.tensor_scalar_add(kv_out[:], kv_bank[:], bias_t[:])
+                nc.scalar.copy(xn_out[:], xn_bank[:])
+            nc.sync.dma_start(out[0:KV, cols], kv_out[:])
             nc.sync.dma_start(out[KV : KV + C, cols], xn_out[:])

@@ -7,9 +7,9 @@ C, S, KV, N = 128, 4096, 128, 2048
 EPS = 1e-5
 INV_STD = 1.0 / math.sqrt(1.0 + EPS)
 
-PIECE = 512
-N_PIECES = N // PIECE
-PIECE_COLS = PIECE // 16
+BANK = 512
+PIECES = (BANK // 2, BANK // 2, BANK, BANK, BANK // 2, BANK // 2)
+assert sum(PIECES) == N
 CHUNK = 1024
 N_CHUNKS = S // CHUNK
 
@@ -24,8 +24,8 @@ def tile_pointnet2msg_kernel(tc, img, gamma, beta, w_kv, b_kv, offs, out):
     nc = tc.nc
     with (
         tc.tile_pool(name="held", bufs=1) as held,
-        tc.tile_pool(name="staged", bufs=N_PIECES) as staged,
-        tc.psum_pool(name="banks", bufs=N_PIECES) as banks,
+        tc.tile_pool(name="staged", bufs=len(PIECES)) as staged,
+        tc.psum_pool(name="banks", bufs=4) as banks,
     ):
         gamma_t = held.tile([C, 1], F32, name="gamma_t")
         beta_t = held.tile([C, 1], F32, name="beta_t")
@@ -58,17 +58,19 @@ def tile_pointnet2msg_kernel(tc, img, gamma, beta, w_kv, b_kv, offs, out):
                 xn[:, k * CHUNK : (k + 1) * CHUNK], raw[k][:], scale_t[:], beta_t[:], MULT, ADD
             )
 
-        for j in range(N_PIECES):
-            picked_cols = xn[:].indirect(offsets[:, j * PIECE_COLS : (j + 1) * PIECE_COLS])
-            cols = slice(j * PIECE, (j + 1) * PIECE)
+        first = 0
+        for j, piece in enumerate(PIECES):
+            picked_cols = xn[:].indirect(offsets[:, first // 16 : (first + piece) // 16])
+            cols = slice(first, first + piece)
+            first += piece
 
-            kv_bank = banks.tile([KV, PIECE], F32, name="kv_bank")
-            xn_bank = banks.tile([C, PIECE], F32, name="xn_bank")
+            kv_bank = banks.tile([KV, piece], F32, name="kv_bank")
+            xn_bank = banks.tile([C, piece], F32, name="xn_bank")
             nc.tensor.matmul(kv_bank[:], weights[:], picked_cols, start=True, stop=True)
             nc.tensor.matmul(xn_bank[:], identity[:], picked_cols, start=True, stop=True)
 
-            kv_out = staged.tile([KV, PIECE], F32, name="kv_out")
-            xn_out = staged.tile([C, PIECE], F32, name="xn_out")
+            kv_out = staged.tile([KV, piece], F32, name="kv_out")
+            xn_out = staged.tile([C, piece], F32, name="xn_out")
             if j % 2 == 0:
                 nc.scalar.activation(kv_out[:], kv_bank[:], IDENTITY, bias=bias_t[:])
                 nc.vector.tensor_copy(xn_out[:], xn_bank[:])

@@ -7,9 +7,9 @@ C, S, KV, N = 128, 4096, 128, 2048
 EPS = 1e-5
 INV_STD = 1.0 / math.sqrt(1.0 + EPS)
 
-BANK = 512
-PIECES = (BANK // 2, BANK // 2, BANK, BANK, BANK // 2, BANK // 2)
-assert sum(PIECES) == N
+PIECE = 512
+N_PIECES = N // PIECE
+PIECE_COLS = PIECE // 16
 CHUNK = 1024
 N_CHUNKS = S // CHUNK
 
@@ -24,13 +24,14 @@ def tile_pointnet2msg_kernel(tc, img, gamma, beta, w_kv, b_kv, offs, out):
     nc = tc.nc
     with (
         tc.tile_pool(name="held", bufs=1) as held,
-        tc.tile_pool(name="staged", bufs=len(PIECES)) as staged,
-        tc.psum_pool(name="banks", bufs=4) as banks,
+        tc.tile_pool(name="staged", bufs=N_PIECES) as staged,
+        tc.psum_pool(name="banks", bufs=3) as banks,
+        tc.psum_pool(name="spread", bufs=1) as spread,
     ):
-        gamma_t = held.tile([C, 1], F32, name="gamma_t")
-        beta_t = held.tile([C, 1], F32, name="beta_t")
-        nc.scalar.dma_start(gamma_t[:], gamma)
-        nc.scalar.dma_start(beta_t[:], beta)
+        rows = held.tile([1, 3 * C], F32, name="rows")
+        nc.scalar.dma_start(rows[:, 0:C], gamma.rearrange("c one -> one c"))
+        nc.sync.dma_start(rows[:, C : 2 * C], beta.rearrange("c one -> one c"))
+        nc.scalar.dma_start(rows[:, 2 * C : 3 * C], b_kv.rearrange("m one -> one m"))
 
         raw = []
         for k in range(N_CHUNKS):
@@ -43,39 +44,43 @@ def tile_pointnet2msg_kernel(tc, img, gamma, beta, w_kv, b_kv, offs, out):
         nc.sync.dma_start(offsets[:], offs)
 
         weights = held.tile([C, KV], BF16, name="weights")
-        bias_t = held.tile([KV, 1], F32, name="bias_t")
         nc.gpsimd.dma_start(weights[:], w_kv)
-        nc.gpsimd.dma_start(bias_t[:], b_kv)
 
         identity = held.tile([C, C], BF16, name="identity")
         make_identity(nc, identity[:])
 
+        one = held.tile([1, 1], F32, name="one")
+        nc.vector.memset(one[:], 1.0)
+        columns = spread.tile([C, 3], F32, name="columns")
+        for i in range(3):
+            nc.tensor.matmul(
+                columns[:, i : i + 1], rows[:, i * C : (i + 1) * C], one[:], start=True, stop=True
+            )
+
         scale_t = held.tile([C, 1], F32, name="scale_t")
-        nc.vector.tensor_scalar_mul(scale_t[:], gamma_t[:], INV_STD)
+        nc.vector.tensor_scalar_mul(scale_t[:], columns[:, 0:1], INV_STD)
+        beta_t = held.tile([C, 1], F32, name="beta_t")
+        nc.vector.tensor_copy(beta_t[:], columns[:, 1:2])
+        bias_t = held.tile([KV, 1], F32, name="bias_t")
+        nc.vector.tensor_copy(bias_t[:], columns[:, 2:3])
         xn = held.tile([C, S], BF16, name="xn")
         for k in range(N_CHUNKS):
             nc.vector.tensor_scalar(
                 xn[:, k * CHUNK : (k + 1) * CHUNK], raw[k][:], scale_t[:], beta_t[:], MULT, ADD
             )
 
-        first = 0
-        for j, piece in enumerate(PIECES):
-            picked_cols = xn[:].indirect(offsets[:, first // 16 : (first + piece) // 16])
-            cols = slice(first, first + piece)
-            first += piece
+        for j in range(N_PIECES):
+            picked_cols = xn[:].indirect(offsets[:, j * PIECE_COLS : (j + 1) * PIECE_COLS])
+            cols = slice(j * PIECE, (j + 1) * PIECE)
 
-            kv_bank = banks.tile([KV, piece], F32, name="kv_bank")
-            xn_bank = banks.tile([C, piece], F32, name="xn_bank")
+            kv_bank = banks.tile([KV, PIECE], F32, name="kv_bank")
             nc.tensor.matmul(kv_bank[:], weights[:], picked_cols, start=True, stop=True)
-            nc.tensor.matmul(xn_bank[:], identity[:], picked_cols, start=True, stop=True)
-
-            kv_out = staged.tile([KV, piece], F32, name="kv_out")
-            xn_out = staged.tile([C, piece], F32, name="xn_out")
-            if j % 2 == 0:
-                nc.scalar.activation(kv_out[:], kv_bank[:], IDENTITY, bias=bias_t[:])
-                nc.vector.tensor_copy(xn_out[:], xn_bank[:])
-            else:
-                nc.vector.tensor_scalar_add(kv_out[:], kv_bank[:], bias_t[:])
-                nc.scalar.copy(xn_out[:], xn_bank[:])
+            kv_out = staged.tile([KV, PIECE], F32, name="kv_out")
+            nc.scalar.activation(kv_out[:], kv_bank[:], IDENTITY, bias=bias_t[:])
             nc.sync.dma_start(out[0:KV, cols], kv_out[:])
+
+            xn_bank = banks.tile([C, PIECE], F32, name="xn_bank")
+            nc.tensor.matmul(xn_bank[:], identity[:], picked_cols, start=True, stop=True)
+            xn_out = staged.tile([C, PIECE], F32, name="xn_out")
+            nc.vector.tensor_copy(xn_out[:], xn_bank[:])
             nc.sync.dma_start(out[KV : KV + C, cols], xn_out[:])

@@ -25,7 +25,7 @@ def tile_pointnet2msg_kernel(tc, img, gamma, beta, w_kv, b_kv, offs, out):
     with (
         tc.tile_pool(name="held", bufs=1) as held,
         tc.tile_pool(name="staged", bufs=N_PIECES) as staged,
-        tc.psum_pool(name="banks", bufs=3) as banks,
+        tc.psum_pool(name="banks", bufs=7) as banks,
         tc.psum_pool(name="spread", bufs=1) as spread,
     ):
         rows = held.tile([1, 3 * C], F32, name="rows")
@@ -73,13 +73,13 @@ def tile_pointnet2msg_kernel(tc, img, gamma, beta, w_kv, b_kv, offs, out):
             picked_cols = xn[:].indirect(offsets[:, j * PIECE_COLS : (j + 1) * PIECE_COLS])
             cols = slice(j * PIECE, (j + 1) * PIECE)
 
-            kv_bank = banks.tile([KV, PIECE], F32, name="kv_bank")
+            kv_bank = banks.tile([KV, PIECE], F32, name="kv_bank", tag="product")
             nc.tensor.matmul(kv_bank[:], weights[:], picked_cols, start=True, stop=True)
             kv_out = staged.tile([KV, PIECE], F32, name="kv_out")
             nc.scalar.activation(kv_out[:], kv_bank[:], IDENTITY, bias=bias_t[:])
             nc.sync.dma_start(out[0:KV, cols], kv_out[:])
 
-            xn_bank = banks.tile([C, PIECE], F32, name="xn_bank")
+            xn_bank = banks.tile([C, PIECE], F32, name="xn_bank", tag="product")
             nc.tensor.matmul(xn_bank[:], identity[:], picked_cols, start=True, stop=True)
             xn_out = staged.tile([C, PIECE], F32, name="xn_out")
             nc.vector.tensor_copy(xn_out[:], xn_bank[:])

@@ -25,7 +25,7 @@ def tile_pointnet2msg_kernel(tc, img, gamma, beta, w_kv, b_kv, offs, out):
     with (
         tc.tile_pool(name="held", bufs=1) as held,
         tc.tile_pool(name="staged", bufs=N_PIECES) as staged,
-        tc.psum_pool(name="banks", bufs=7) as banks,
+        tc.psum_pool(name="banks", bufs=6) as banks,
         tc.psum_pool(name="spread", bufs=1) as spread,
     ):
         rows = held.tile([1, 3 * C], F32, name="rows")
@@ -51,23 +51,27 @@ def tile_pointnet2msg_kernel(tc, img, gamma, beta, w_kv, b_kv, offs, out):
 
         one = held.tile([1, 1], F32, name="one")
         nc.vector.memset(one[:], 1.0)
-        columns = spread.tile([C, 3], F32, name="columns")
-        for i in range(3):
-            nc.tensor.matmul(
-                columns[:, i : i + 1], rows[:, i * C : (i + 1) * C], one[:], start=True, stop=True
-            )
 
+        def spread_row(column, i):
+            nc.tensor.matmul(column, rows[:, i * C : (i + 1) * C], one[:], start=True, stop=True)
+
+        norm_columns = spread.tile([C, 2], F32, name="norm_columns")
+        spread_row(norm_columns[:, 0:1], 0)
+        spread_row(norm_columns[:, 1:2], 1)
         scale_t = held.tile([C, 1], F32, name="scale_t")
-        nc.vector.tensor_scalar_mul(scale_t[:], columns[:, 0:1], INV_STD)
+        nc.vector.tensor_scalar_mul(scale_t[:], norm_columns[:, 0:1], INV_STD)
         beta_t = held.tile([C, 1], F32, name="beta_t")
-        nc.vector.tensor_copy(beta_t[:], columns[:, 1:2])
-        bias_t = held.tile([KV, 1], F32, name="bias_t")
-        nc.vector.tensor_copy(bias_t[:], columns[:, 2:3])
+        nc.vector.tensor_copy(beta_t[:], norm_columns[:, 1:2])
         xn = held.tile([C, S], BF16, name="xn")
         for k in range(N_CHUNKS):
             nc.vector.tensor_scalar(
                 xn[:, k * CHUNK : (k + 1) * CHUNK], raw[k][:], scale_t[:], beta_t[:], MULT, ADD
             )
+
+        bias_column = spread.tile([KV, 1], F32, name="bias_column")
+        spread_row(bias_column[:], 2)
+        bias_t = held.tile([KV, 1], F32, name="bias_t")
+        nc.vector.tensor_copy(bias_t[:], bias_column[:])
 
         for j in range(N_PIECES):
             picked_cols = xn[:].indirect(offsets[:, j * PIECE_COLS : (j + 1) * PIECE_COLS])

@@ -36,8 +36,7 @@ def tile_pointnet2msg_kernel(tc, img, gamma, beta, w_kv, b_kv, offs, out):
         raw = []
         for k in range(N_CHUNKS):
             chunk = held.tile([C, CHUNK], BF16, name=f"raw{k}")
-            queue = nc.sync if k % 2 == 0 else nc.scalar
-            queue.dma_start(chunk[:], img[:, k * CHUNK : (k + 1) * CHUNK])
+            nc.sync.dma_start(chunk[:], img[:, k * CHUNK : (k + 1) * CHUNK])
             raw.append(chunk)
 
         offsets = held.tile([128, N // 16], U16, name="offsets")

import math

import concourse.mybir as mybir
from concourse.masks import make_identity

C, S, KV, N = 128, 4096, 128, 2048
EPS = 1e-5
INV_STD = 1.0 / math.sqrt(1.0 + EPS)

PIECE = 512
N_PIECES = N // PIECE
PIECE_COLS = PIECE // 16
CHUNK = 1024
N_CHUNKS = S // CHUNK

FLOPS = 2 * C * KV * N

BF16, F32, U16 = mybir.dt.bfloat16, mybir.dt.float32, mybir.dt.uint16
MULT, ADD = mybir.AluOpType.mult, mybir.AluOpType.add
IDENTITY = mybir.ActivationFunctionType.Identity


def tile_pointnet2msg_kernel(tc, img, gamma, beta, w_kv, b_kv, offs, out):
    nc = tc.nc
    with (
        tc.tile_pool(name="held", bufs=1) as held,
        tc.tile_pool(name="staged", bufs=N_PIECES) as staged,
        tc.psum_pool(name="banks", bufs=6) as banks,
        tc.psum_pool(name="spread", bufs=1) as spread,
    ):
        rows = held.tile([1, 3 * C], F32, name="rows")
        nc.scalar.dma_start(rows[:, 0:C], gamma.rearrange("c one -> one c"))
        nc.sync.dma_start(rows[:, C : 2 * C], beta.rearrange("c one -> one c"))
        nc.scalar.dma_start(rows[:, 2 * C : 3 * C], b_kv.rearrange("m one -> one m"))

        raw = []
        for k in range(N_CHUNKS):
            chunk = held.tile([C, CHUNK], BF16, name=f"raw{k}")
            nc.sync.dma_start(chunk[:], img[:, k * CHUNK : (k + 1) * CHUNK])
            raw.append(chunk)

        offsets = held.tile([128, N // 16], U16, name="offsets")
        nc.sync.dma_start(offsets[:], offs)

        weights = held.tile([C, KV], BF16, name="weights")
        nc.gpsimd.dma_start(weights[:], w_kv)

        identity = held.tile([C, C], BF16, name="identity")
        make_identity(nc, identity[:])

        one = held.tile([1, 1], F32, name="one")
        nc.vector.memset(one[:], 1.0)

        def spread_row(column, i):
            nc.tensor.matmul(column, rows[:, i * C : (i + 1) * C], one[:], start=True, stop=True)

        norm_columns = spread.tile([C, 2], F32, name="norm_columns")
        spread_row(norm_columns[:, 0:1], 0)
        spread_row(norm_columns[:, 1:2], 1)
        scale_t = held.tile([C, 1], F32, name="scale_t")
        nc.vector.tensor_scalar_mul(scale_t[:], norm_columns[:, 0:1], INV_STD)
        beta_t = held.tile([C, 1], F32, name="beta_t")
        nc.vector.tensor_copy(beta_t[:], norm_columns[:, 1:2])
        xn = held.tile([C, S], BF16, name="xn")
        for k in range(N_CHUNKS):
            nc.vector.tensor_scalar(
                xn[:, k * CHUNK : (k + 1) * CHUNK], raw[k][:], scale_t[:], beta_t[:], MULT, ADD
            )

        bias_column = spread.tile([KV, 1], F32, name="bias_column")
        spread_row(bias_column[:], 2)
        bias_t = held.tile([KV, 1], F32, name="bias_t")
        nc.vector.tensor_copy(bias_t[:], bias_column[:])

        for j in range(N_PIECES):
            picked_cols = xn[:].indirect(offsets[:, j * PIECE_COLS : (j + 1) * PIECE_COLS])
            cols = slice(j * PIECE, (j + 1) * PIECE)

            kv_bank = banks.tile([KV, PIECE], F32, name="kv_bank", tag="product")
            nc.tensor.matmul(kv_bank[:], weights[:], picked_cols, start=True, stop=True)
            kv_out = staged.tile([KV, PIECE], F32, name="kv_out")
            nc.scalar.activation(kv_out[:], kv_bank[:], IDENTITY, bias=bias_t[:])
            nc.sync.dma_start(out[0:KV, cols], kv_out[:])

            xn_bank = banks.tile([C, PIECE], F32, name="xn_bank", tag="product")
            nc.tensor.matmul(xn_bank[:], identity[:], picked_cols, start=True, stop=True)
            xn_out = staged.tile([C, PIECE], F32, name="xn_out")
            nc.vector.tensor_copy(xn_out[:], xn_bank[:])
            nc.sync.dma_start(out[KV : KV + C, cols], xn_out[:])
